import numpy as np
import ml_dtypes


def mxq(x, axis, fmt="e4m3"):
    dtype, down = {"e4m3": (ml_dtypes.float8_e4m3fn, 7), "e5m2": (ml_dtypes.float8_e5m2, 14)}[fmt]
    v = np.moveaxis(np.asarray(x, np.float32).astype(ml_dtypes.bfloat16).astype(np.float64), axis, -1)
    blocks = v.reshape(v.shape[:-1] + (-1, 32))
    amax = np.abs(blocks).max(-1, keepdims=True)
    byte = np.maximum(np.where(amax > 0, np.frexp(amax)[1] - 1 + 127, 0) - down, 1)
    scale = np.exp2(byte - 127.0)
    codes = (blocks / scale).astype(np.float32).astype(dtype).astype(np.float64)
    return np.moveaxis((codes * scale).reshape(v.shape), -1, axis)


WIDE = False


def mx_kscale(k):
    if not WIDE:
        return np.ones(k)
    levels = np.array([10, -10, 5, -5, 0])
    a = np.random.permutation(np.resize(levels, k // 512 * 4)).reshape(k // 512, 4)
    idx = np.arange(k)
    return np.exp2(a[idx // 512, idx % 128 // 32])


BF16 = ml_dtypes.bfloat16


def bf(x):
    return np.asarray(x, np.float32).astype(BF16)


def f64(x):
    return np.asarray(x).astype(np.float64)


B, IN, H = 128, 512, 512


def sigmoid(v):
    return 1.0 / (1.0 + np.exp(-v))


def setup_inputs():
    s, t = mx_kscale(IN), mx_kscale(H)
    a = np.sqrt(2.0 / (IN + H))
    d = 0.3 + np.random.standard_normal((B, H)) * 1.6
    return {
        "x": bf(np.random.standard_normal((B, IN)) * s),
        "h_prev": bf(np.random.standard_normal((B, H)) * t),
        "c_prev": bf(np.random.standard_normal((B, H))),
        "n_prev": bf(1.0 + np.random.standard_normal((B, H)) * 0.1),
        "i_prime": bf(np.exp(np.minimum(d, 0.0))),
        "f_prime": bf(np.exp(np.minimum(-d, 0.0))),
        "Wz_x": bf(np.random.standard_normal((H, IN)) * a / s),
        "b_z": bf(np.random.standard_normal(H) * 0.3),
        "Wz_h": bf(np.random.standard_normal((H, H)) * a / t),
        "Wo_x": bf(np.random.standard_normal((H, IN)) * a / s),
        "b_o": bf(np.random.standard_normal(H) * 0.3),
        "Wo_h": bf(np.random.standard_normal((H, H)) * a / t),
    }


def reference(x, h_prev, c_prev, n_prev, i_prime, f_prime, Wz_x, b_z, Wz_h, Wo_x, b_o, Wo_h):
    xq = mxq(f64(x), 1, "e4m3")
    hq = mxq(f64(h_prev), 1, "e4m3")
    z_aff = (xq @ mxq(f64(Wz_x), 1, "e4m3").T) + f64(b_z) + (hq @ mxq(f64(Wz_h), 1, "e4m3").T)
    o_aff = (xq @ mxq(f64(Wo_x), 1, "e4m3").T) + f64(b_o) + (hq @ mxq(f64(Wo_h), 1, "e4m3").T)
    z = np.tanh(z_aff)
    c_t = f64(f_prime) * f64(c_prev) + f64(i_prime) * z
    n_t = f64(f_prime) * f64(n_prev) + f64(i_prime)
    h_t = sigmoid(o_aff) * (c_t / np.maximum(n_t, 1e-6))
    return h_t, c_t

@@ -1,0 +1,149 @@
+from contextlib import ExitStack
+
+import concourse.mybir as mybir
+from concourse.masks import make_identity
+
+F32 = mybir.dt.float32
+BF16 = mybir.dt.bfloat16
+U32 = mybir.dt.uint32
+U8 = mybir.dt.uint8
+FP8X4 = mybir.dt.float8_e4m3fn_x4
+ALU = mybir.AluOpType
+ACT = mybir.ActivationFunctionType
+
+P = 128
+K = 512
+H = 512
+WORDS = K // 2
+BLOCKS = H // P
+
+FLOPS = 2 * P * (2 * K) * (2 * H)
+
+
+def quantise_two_blocks(nc, flip, stage, ident, words, first_block, codes, scales):
+    bank = flip.tile([P, 2 * WORDS], F32)
+    for piece in range(4):
+        source = first_block * WORDS + piece * P
+        nc.tensor.transpose(
+            bank[:, piece * P : (piece + 1) * P], words[:, source : source + P], ident[:]
+        )
+    grouped = stage.tile([P, 4 * 2 * P], BF16, align_bytes=64)
+    nc.scalar.copy(
+        out=grouped[:].bitcast(F32).rearrange("q (s c u) -> q s c u", s=2, u=2),
+        in_=bank[:].rearrange("q (s u c) -> q s c u", s=2, u=2),
+    )
+    nc.vector.quantize_mx(out=codes.bitcast(FP8X4), scales=scales, in_=grouped[:])
+
+
+def tile_slstmlayer_pb_s_kernel(
+    tc, x, h_prev, c_prev, n_prev, i_prime, f_prime, Wz_x, b_z, Wz_h, Wo_x, b_o, Wo_h, out_0, out_1
+):
+    nc = tc.nc
+    with ExitStack() as ctx:
+        keep = ctx.enter_context(tc.tile_pool(name="keep", bufs=1))
+        stage = ctx.enter_context(tc.tile_pool(name="stage", bufs=4))
+        flip = ctx.enter_context(tc.psum_pool(name="flip", bufs=4))
+        sums = ctx.enter_context(tc.psum_pool(name="sums", bufs=1))
+
+        ident = keep.tile([P, P], F32)
+        make_identity(nc, ident[:])
+
+        def load_rows(name, source):
+            rows = keep.tile([P, H], BF16, name=name)
+            nc.sync.dma_start(out=rows[:], in_=source)
+            return rows
+
+        f_sb = load_rows("f_sb", f_prime)
+        n_sb = load_rows("n_sb", n_prev)
+        i_sb = load_rows("i_sb", i_prime)
+
+        acts = keep.tile([P, 2 * K], BF16)
+        nc.sync.dma_start(out=acts[:, 0:K], in_=x)
+        nc.sync.dma_start(out=acts[:, K : 2 * K], in_=h_prev)
+
+        def load_weight(name, source):
+            rows = keep.tile([P, BLOCKS * K], BF16, name=name)
+            nc.sync.dma_start(out=rows[:], in_=source.rearrange("(p t) k -> p (t k)", t=BLOCKS))
+            return rows
+
+        weights = {}
+        weights["z", "x"] = load_weight("wzx", Wz_x)
+        weights["z", "h"] = load_weight("wzh", Wz_h)
+        c_sb = load_rows("c_sb", c_prev)
+        weights["o", "x"] = load_weight("wox", Wo_x)
+        weights["o", "h"] = load_weight("woh", Wo_h)
+
+        bias = {}
+        for gate, source in (("z", b_z), ("o", b_o)):
+            bias[gate] = keep.tile([P, H], BF16, name="bias_" + gate)
+            nc.scalar.dma_start(out=bias[gate][:], in_=source.partition_broadcast(P))
+
+        n_t = keep.tile([P, H], F32)
+        nc.vector.tensor_tensor(out=n_t[:], in0=f_sb[:], in1=n_sb[:], op=ALU.mult)
+        nc.vector.tensor_tensor(out=n_t[:], in0=n_t[:], in1=i_sb[:], op=ALU.add)
+        nc.vector.tensor_scalar_max(out=n_t[:], in0=n_t[:], scalar1=1e-6)
+        n_inverse = keep.tile([P, H], F32)
+        nc.vector.reciprocal(out=n_inverse[:], in_=n_t[:])
+
+        act_codes = keep.tile([P, 2 * P], U32, align_bytes=64)
+        act_scales = keep.tile([P, 2 * P], U8, align_bytes=64)
+        quantise_two_blocks(
+            nc, flip, stage, ident, acts[:].bitcast(F32), 0, act_codes[:], act_scales[:]
+        )
+        act_columns = {"x": slice(0, P), "h": slice(P, 2 * P)}
+
+        def gate_sums(gate):
+            acc = sums.tile([P, H], F32, name="acc_" + gate)
+            for side in ("x", "h"):
+                codes = keep.tile([P, H], U32, name="codes_" + gate + side, align_bytes=64)
+                scales = keep.tile([P, H], U8, name="scales_" + gate + side, align_bytes=64)
+                words = weights[gate, side][:].bitcast(F32)
+                for first_block in range(0, BLOCKS, 2):
+                    columns = slice(first_block * P, (first_block + 2) * P)
+                    quantise_two_blocks(
+                        nc, flip, stage, ident, words, first_block,
+                        codes[:, columns], scales[:, columns],
+                    )
+                nc.tensor.matmul_mx(
+                    out=acc[:],
+                    lhsT=act_codes[:, act_columns[side]].bitcast(FP8X4),
+                    lhsT_scale=act_scales[:, act_columns[side]],
+                    rhs=codes[:].bitcast(FP8X4),
+                    rhs_scale=scales[:],
+                    start=(side == "x"),
+                    stop=(side == "h"),
+                )
+            return acc
+
+        def add_bias(gate, acc):
+            affine = keep.tile([P, H], F32, name="affine_" + gate)
+            nc.vector.tensor_tensor(
+                out=affine[:].rearrange("b (p t) -> b p t", t=BLOCKS),
+                in0=acc[:].rearrange("b (t p) -> b p t", t=BLOCKS),
+                in1=bias[gate][:].rearrange("b (p t) -> b p t", t=BLOCKS),
+                op=ALU.add,
+            )
+            return affine
+
+        z_affine = add_bias("z", gate_sums("z"))
+        z = keep.tile([P, H], F32)
+        nc.scalar.activation(out=z[:], in_=z_affine[:], func=ACT.Tanh)
+        kept_cell = keep.tile([P, H], F32)
+        nc.vector.tensor_tensor(out=kept_cell[:], in0=f_sb[:], in1=c_sb[:], op=ALU.mult)
+        c_t = keep.tile([P, H], F32)
+        nc.vector.tensor_tensor(out=c_t[:], in0=i_sb[:], in1=z[:], op=ALU.mult)
+        nc.vector.tensor_tensor(out=c_t[:], in0=c_t[:], in1=kept_cell[:], op=ALU.add)
+        nc.sync.dma_start(out=out_1, in_=c_t[:])
+
+        half_ratio = keep.tile([P, H], F32)
+        nc.vector.scalar_tensor_tensor(
+            out=half_ratio[:], in0=c_t[:], scalar=0.5, in1=n_inverse[:], op0=ALU.mult, op1=ALU.mult
+        )
+        o_affine = add_bias("o", gate_sums("o"))
+        o_tanh = keep.tile([P, H], F32)
+        nc.scalar.activation(out=o_tanh[:], in_=o_affine[:], func=ACT.Tanh, scale=0.5)
+        h_t = keep.tile([P, H], F32)
+        nc.vector.scalar_tensor_tensor(
+            out=h_t[:], in0=o_tanh[:], scalar=1.0, in1=half_ratio[:], op0=ALU.add, op1=ALU.mult
+        )
+        nc.sync.dma_start(out=out_0, in_=h_t[:])

@@ -82,8 +82,10 @@ def tile_slstmlayer_pb_s_kernel(
         nc.vector.tensor_tensor(out=n_t[:], in0=f_sb[:], in1=n_sb[:], op=ALU.mult)
         nc.vector.tensor_tensor(out=n_t[:], in0=n_t[:], in1=i_sb[:], op=ALU.add)
         nc.vector.tensor_scalar_max(out=n_t[:], in0=n_t[:], scalar1=1e-6)
+        log_n = keep.tile([P, H], F32)
+        nc.scalar.activation(out=log_n[:], in_=n_t[:], func=ACT.Ln)
         n_inverse = keep.tile([P, H], F32)
-        nc.vector.reciprocal(out=n_inverse[:], in_=n_t[:])
+        nc.scalar.activation(out=n_inverse[:], in_=log_n[:], func=ACT.Exp, scale=-1.0)
 
         act_codes = keep.tile([P, 2 * P], U32, align_bytes=64)
         act_scales = keep.tile([P, 2 * P], U8, align_bytes=64)

@@ -15,20 +15,20 @@ P = 128
 K = 512
 H = 512
 WORDS = K // 2
-BLOCKS = H // P
+HALF = 2 * P
 
 FLOPS = 2 * P * (2 * K) * (2 * H)
 
 
-def quantise_two_blocks(nc, flip, stage, ident, words, first_block, codes, scales):
+def quantise_two_blocks(nc, copy, flip, stage, ident, words, first_block, codes, scales):
     bank = flip.tile([P, 2 * WORDS], F32)
     for piece in range(4):
         source = first_block * WORDS + piece * P
         nc.tensor.transpose(
             bank[:, piece * P : (piece + 1) * P], words[:, source : source + P], ident[:]
         )
-    grouped = stage.tile([P, 4 * 2 * P], BF16, align_bytes=64)
-    nc.scalar.copy(
+    grouped = stage.tile([P, 4 * HALF], BF16, align_bytes=64)
+    copy(
         out=grouped[:].bitcast(F32).rearrange("q (s c u) -> q s c u", s=2, u=2),
         in_=bank[:].rearrange("q (s u c) -> q s c u", s=2, u=2),
     )
@@ -39,14 +39,23 @@ def tile_slstmlayer_pb_s_kernel(
     tc, x, h_prev, c_prev, n_prev, i_prime, f_prime, Wz_x, b_z, Wz_h, Wo_x, b_o, Wo_h, out_0, out_1
 ):
     nc = tc.nc
+    half_gates = (("z", 0), ("z", 1), ("o", 0), ("o", 1))
+    weights = {("z", "x"): Wz_x, ("z", "h"): Wz_h, ("o", "x"): Wo_x, ("o", "h"): Wo_h}
+    sides = ("x", "h")
+
     with ExitStack() as ctx:
         keep = ctx.enter_context(tc.tile_pool(name="keep", bufs=1))
         stage = ctx.enter_context(tc.tile_pool(name="stage", bufs=4))
-        flip = ctx.enter_context(tc.psum_pool(name="flip", bufs=4))
-        sums = ctx.enter_context(tc.psum_pool(name="sums", bufs=1))
+        flip = ctx.enter_context(tc.psum_pool(name="flip", bufs=6))
+        sums = ctx.enter_context(tc.psum_pool(name="sums", bufs=2))
 
         ident = keep.tile([P, P], F32)
         make_identity(nc, ident[:])
+
+        bias_rows = keep.tile([P, HALF], BF16)
+        nc.vector.memset(bias_rows[:], 0.0)
+        nc.sync.dma_start(out=bias_rows[0:2, :], in_=b_z.rearrange("(r c) -> r c", r=2))
+        nc.sync.dma_start(out=bias_rows[2:4, :], in_=b_o.rearrange("(r c) -> r c", r=2))
 
         def load_rows(name, source):
             rows = keep.tile([P, H], BF16, name=name)
@@ -61,91 +70,121 @@ def tile_slstmlayer_pb_s_kernel(
         nc.sync.dma_start(out=acts[:, 0:K], in_=x)
         nc.sync.dma_start(out=acts[:, K : 2 * K], in_=h_prev)
 
-        def load_weight(name, source):
-            rows = keep.tile([P, BLOCKS * K], BF16, name=name)
-            nc.sync.dma_start(out=rows[:], in_=source.rearrange("(p t) k -> p (t k)", t=BLOCKS))
-            return rows
-
-        weights = {}
-        weights["z", "x"] = load_weight("wzx", Wz_x)
-        weights["z", "h"] = load_weight("wzh", Wz_h)
+        weight_rows = {}
+        for gate, s in half_gates:
+            rows = keep.tile([P, 4 * K], BF16, name="rows_%s%d" % (gate, s))
+            for number, side in enumerate(sides):
+                nc.sync.dma_start(
+                    out=rows[:, number * 2 * K : (number + 1) * 2 * K],
+                    in_=weights[gate, side].rearrange("(s p j) k -> s p (j k)", s=2, j=2)[s],
+                )
+            weight_rows[gate, s] = rows
         c_sb = load_rows("c_sb", c_prev)
-        weights["o", "x"] = load_weight("wox", Wo_x)
-        weights["o", "h"] = load_weight("woh", Wo_h)
 
-        bias = {}
-        for gate, source in (("z", b_z), ("o", b_o)):
-            bias[gate] = keep.tile([P, H], BF16, name="bias_" + gate)
-            nc.scalar.dma_start(out=bias[gate][:], in_=source.partition_broadcast(P))
+        turned = flip.tile([P, 2 * WORDS], F32, tag="bank")
+        nc.tensor.transpose(turned[:, 0:P], bias_rows[:].bitcast(F32), ident[:])
+        bias_words = keep.tile([P, 4], F32)
+        nc.vector.tensor_copy(out=bias_words[:], in_=turned[:, 0:4])
+        spread = flip.tile([P, 2 * WORDS], F32, tag="bank")
+        for r in range(4):
+            nc.tensor.transpose(
+                spread[:, r * P : (r + 1) * P],
+                bias_words[:, r : r + 1].to_broadcast([P, P]),
+                ident[:],
+            )
+        bias_all = keep.tile([P, 2 * H], BF16)
+        nc.scalar.copy(out=bias_all[:].bitcast(F32), in_=spread[:])
+        bias = {"z": bias_all[:, 0:H], "o": bias_all[:, H : 2 * H]}
 
         n_t = keep.tile([P, H], F32)
         nc.vector.tensor_tensor(out=n_t[:], in0=f_sb[:], in1=n_sb[:], op=ALU.mult)
         nc.vector.tensor_tensor(out=n_t[:], in0=n_t[:], in1=i_sb[:], op=ALU.add)
         nc.vector.tensor_scalar_max(out=n_t[:], in0=n_t[:], scalar1=1e-6)
+
+        act_codes = keep.tile([P, HALF], U32, align_bytes=64)
+        act_scales = keep.tile([P, HALF], U8, align_bytes=64)
+        quantise_two_blocks(
+            nc, nc.scalar.copy, flip, stage, ident,
+            acts[:].bitcast(F32), 0, act_codes[:], act_scales[:],
+        )
+
         log_n = keep.tile([P, H], F32)
         nc.scalar.activation(out=log_n[:], in_=n_t[:], func=ACT.Ln)
         n_inverse = keep.tile([P, H], F32)
         nc.scalar.activation(out=n_inverse[:], in_=log_n[:], func=ACT.Exp, scale=-1.0)
 
-        act_codes = keep.tile([P, 2 * P], U32, align_bytes=64)
-        act_scales = keep.tile([P, 2 * P], U8, align_bytes=64)
-        quantise_two_blocks(
-            nc, flip, stage, ident, acts[:].bitcast(F32), 0, act_codes[:], act_scales[:]
-        )
-        act_columns = {"x": slice(0, P), "h": slice(P, 2 * P)}
+        codes = {}
+        scales = {}
 
-        def gate_sums(gate):
-            acc = sums.tile([P, H], F32, name="acc_" + gate)
-            for side in ("x", "h"):
-                codes = keep.tile([P, H], U32, name="codes_" + gate + side, align_bytes=64)
-                scales = keep.tile([P, H], U8, name="scales_" + gate + side, align_bytes=64)
-                words = weights[gate, side][:].bitcast(F32)
-                for first_block in range(0, BLOCKS, 2):
-                    columns = slice(first_block * P, (first_block + 2) * P)
-                    quantise_two_blocks(
-                        nc, flip, stage, ident, words, first_block,
-                        codes[:, columns], scales[:, columns],
-                    )
+        def prepare(gate, s):
+            copy = nc.vector.tensor_copy if (gate, s) == half_gates[0] else nc.scalar.copy
+            codes[gate, s] = keep.tile([P, 2 * HALF], U32, name="codes_%s%d" % (gate, s), align_bytes=64)
+            scales[gate, s] = keep.tile([P, 2 * HALF], U8, name="scales_%s%d" % (gate, s), align_bytes=64)
+            for number in range(len(sides)):
+                columns = slice(number * HALF, (number + 1) * HALF)
+                quantise_two_blocks(
+                    nc, copy, flip, stage, ident,
+                    weight_rows[gate, s][:].bitcast(F32), 2 * number,
+                    codes[gate, s][:, columns], scales[gate, s][:, columns],
+                )
+
+        squashed = {"z": keep.tile([P, H], F32, name="tanh_z"), "o": keep.tile([P, H], F32, name="tanh_o")}
+
+        def squash(gate, s):
+            acc = sums.tile([P, HALF], F32)
+            for number in range(len(sides)):
+                columns = slice(number * HALF, (number + 1) * HALF)
                 nc.tensor.matmul_mx(
                     out=acc[:],
-                    lhsT=act_codes[:, act_columns[side]].bitcast(FP8X4),
-                    lhsT_scale=act_scales[:, act_columns[side]],
-                    rhs=codes[:].bitcast(FP8X4),
-                    rhs_scale=scales[:],
-                    start=(side == "x"),
-                    stop=(side == "h"),
+                    lhsT=act_codes[:, number * P : (number + 1) * P].bitcast(FP8X4),
+                    lhsT_scale=act_scales[:, number * P : (number + 1) * P],
+                    rhs=codes[gate, s][:, columns].bitcast(FP8X4),
+                    rhs_scale=scales[gate, s][:, columns],
+                    start=(number == 0),
+                    stop=(number == len(sides) - 1),
                 )
-            return acc
-
-        def add_bias(gate, acc):
-            affine = keep.tile([P, H], F32, name="affine_" + gate)
+            outputs = slice(s * HALF, (s + 1) * HALF)
+            affine = stage.tile([P, HALF], F32)
             nc.vector.tensor_tensor(
-                out=affine[:].rearrange("b (p t) -> b p t", t=BLOCKS),
-                in0=acc[:].rearrange("b (t p) -> b p t", t=BLOCKS),
-                in1=bias[gate][:].rearrange("b (p t) -> b p t", t=BLOCKS),
+                out=affine[:].rearrange("b (p j) -> b p j", j=2),
+                in0=acc[:].rearrange("b (j p) -> b p j", j=2),
+                in1=bias[gate][:, outputs].rearrange("b (p j) -> b p j", j=2),
                 op=ALU.add,
             )
-            return affine
+            nc.scalar.activation(
+                out=squashed[gate][:, outputs], in_=affine[:], func=ACT.Tanh,
+                scale=(1.0 if gate == "z" else 0.5),
+            )
 
-        z_affine = add_bias("z", gate_sums("z"))
-        z = keep.tile([P, H], F32)
-        nc.scalar.activation(out=z[:], in_=z_affine[:], func=ACT.Tanh)
-        kept_cell = keep.tile([P, H], F32)
-        nc.vector.tensor_tensor(out=kept_cell[:], in0=f_sb[:], in1=c_sb[:], op=ALU.mult)
         c_t = keep.tile([P, H], F32)
-        nc.vector.tensor_tensor(out=c_t[:], in0=i_sb[:], in1=z[:], op=ALU.mult)
-        nc.vector.tensor_tensor(out=c_t[:], in0=c_t[:], in1=kept_cell[:], op=ALU.add)
-        nc.sync.dma_start(out=out_1, in_=c_t[:])
-
         half_ratio = keep.tile([P, H], F32)
-        nc.vector.scalar_tensor_tensor(
-            out=half_ratio[:], in0=c_t[:], scalar=0.5, in1=n_inverse[:], op0=ALU.mult, op1=ALU.mult
-        )
-        o_affine = add_bias("o", gate_sums("o"))
-        o_tanh = keep.tile([P, H], F32)
-        nc.scalar.activation(out=o_tanh[:], in_=o_affine[:], func=ACT.Tanh, scale=0.5)
         h_t = keep.tile([P, H], F32)
-        nc.vector.scalar_tensor_tensor(
-            out=h_t[:], in0=o_tanh[:], scalar=1.0, in1=half_ratio[:], op0=ALU.add, op1=ALU.mult
-        )
-        nc.sync.dma_start(out=out_0, in_=h_t[:])
+
+        def finish(gate, s):
+            outputs = slice(s * HALF, (s + 1) * HALF)
+            if gate == "z":
+                kept = stage.tile([P, HALF], F32)
+                nc.vector.tensor_tensor(out=kept[:], in0=f_sb[:, outputs], in1=c_sb[:, outputs], op=ALU.mult)
+                fresh = stage.tile([P, HALF], F32)
+                nc.vector.tensor_tensor(out=fresh[:], in0=i_sb[:, outputs], in1=squashed["z"][:, outputs], op=ALU.mult)
+                nc.vector.tensor_tensor(out=c_t[:, outputs], in0=kept[:], in1=fresh[:], op=ALU.add)
+                nc.sync.dma_start(out=out_1[:, outputs], in_=c_t[:, outputs])
+                nc.vector.scalar_tensor_tensor(
+                    out=half_ratio[:, outputs], in0=c_t[:, outputs], scalar=0.5,
+                    in1=n_inverse[:, outputs], op0=ALU.mult, op1=ALU.mult,
+                )
+            else:
+                nc.vector.scalar_tensor_tensor(
+                    out=h_t[:, outputs], in0=squashed["o"][:, outputs], scalar=1.0,
+                    in1=half_ratio[:, outputs], op0=ALU.add, op1=ALU.mult,
+                )
+                nc.sync.dma_start(out=out_0[:, outputs], in_=h_t[:, outputs])
+
+        count = len(half_gates)
+        for step in range(-1, count + 1):
+            if step + 1 < count:
+                prepare(*half_gates[step + 1])
+            if 0 <= step < count:
+                squash(*half_gates[step])
+            if step >= 1:
+                finish(*half_gates[step - 1])

@@ -16,11 +16,12 @@ K = 512
 H = 512
 WORDS = K // 2
 HALF = 2 * P
+QUARTERS = 4
 
 FLOPS = 2 * P * (2 * K) * (2 * H)
 
 
-def quantise_two_blocks(nc, copy, flip, stage, ident, words, first_block, codes, scales):
+def flip_two_blocks(nc, flip, stage, ident, words, first_block):
     bank = flip.tile([P, 2 * WORDS], F32)
     for piece in range(4):
         source = first_block * WORDS + piece * P
@@ -28,11 +29,11 @@ def quantise_two_blocks(nc, copy, flip, stage, ident, words, first_block, codes,
             bank[:, piece * P : (piece + 1) * P], words[:, source : source + P], ident[:]
         )
     grouped = stage.tile([P, 4 * HALF], BF16, align_bytes=64)
-    copy(
+    nc.scalar.copy(
         out=grouped[:].bitcast(F32).rearrange("q (s c u) -> q s c u", s=2, u=2),
         in_=bank[:].rearrange("q (s u c) -> q s c u", s=2, u=2),
     )
-    nc.vector.quantize_mx(out=codes.bitcast(FP8X4), scales=scales, in_=grouped[:])
+    return grouped
 
 
 def tile_slstmlayer_pb_s_kernel(
@@ -48,12 +49,13 @@ def tile_slstmlayer_pb_s_kernel(
         stage = ctx.enter_context(tc.tile_pool(name="stage", bufs=4))
         flip = ctx.enter_context(tc.psum_pool(name="flip", bufs=6))
         sums = ctx.enter_context(tc.psum_pool(name="sums", bufs=2))
+        ctx.enter_context(tc.manual_schedule())
 
+        bias_rows = keep.tile([P, HALF], BF16)
+        nc.gpsimd.memset(bias_rows[:].bitcast(F32), 0.0)
         ident = keep.tile([P, P], F32)
         make_identity(nc, ident[:])
 
-        bias_rows = keep.tile([P, HALF], BF16)
-        nc.vector.memset(bias_rows[:], 0.0)
         nc.sync.dma_start(out=bias_rows[0:2, :], in_=b_z.rearrange("(r c) -> r c", r=2))
         nc.sync.dma_start(out=bias_rows[2:4, :], in_=b_o.rearrange("(r c) -> r c", r=2))
 
@@ -79,7 +81,8 @@ def tile_slstmlayer_pb_s_kernel(
                     in_=weights[gate, side].rearrange("(s p j) k -> s p (j k)", s=2, j=2)[s],
                 )
             weight_rows[gate, s] = rows
-        c_sb = load_rows("c_sb", c_prev)
+            if (gate, s) == ("z", 1):
+                c_sb = load_rows("c_sb", c_prev)
 
         turned = flip.tile([P, 2 * WORDS], F32, tag="bank")
         nc.tensor.transpose(turned[:, 0:P], bias_rows[:].bitcast(F32), ident[:])
@@ -100,35 +103,49 @@ def tile_slstmlayer_pb_s_kernel(
         nc.vector.tensor_tensor(out=n_t[:], in0=f_sb[:], in1=n_sb[:], op=ALU.mult)
         nc.vector.tensor_tensor(out=n_t[:], in0=n_t[:], in1=i_sb[:], op=ALU.add)
         nc.vector.tensor_scalar_max(out=n_t[:], in0=n_t[:], scalar1=1e-6)
+        n_inverse = keep.tile([P, H], F32)
+
+        def invert(quarter):
+            columns = slice(quarter * H // QUARTERS, (quarter + 1) * H // QUARTERS)
+            nc.vector.reciprocal(out=n_inverse[:, columns], in_=n_t[:, columns])
+
+        invert(0)
 
         act_codes = keep.tile([P, HALF], U32, align_bytes=64)
         act_scales = keep.tile([P, HALF], U8, align_bytes=64)
-        quantise_two_blocks(
-            nc, nc.scalar.copy, flip, stage, ident,
-            acts[:].bitcast(F32), 0, act_codes[:], act_scales[:],
+        act_grouped = flip_two_blocks(nc, flip, stage, ident, acts[:].bitcast(F32), 0)
+        nc.vector.quantize_mx(
+            out=act_codes[:].bitcast(FP8X4), scales=act_scales[:], in_=act_grouped[:]
         )
 
-        log_n = keep.tile([P, H], F32)
-        nc.scalar.activation(out=log_n[:], in_=n_t[:], func=ACT.Ln)
-        n_inverse = keep.tile([P, H], F32)
-        nc.scalar.activation(out=n_inverse[:], in_=log_n[:], func=ACT.Exp, scale=-1.0)
-
+        grouped = {}
         codes = {}
         scales = {}
 
-        def prepare(gate, s):
-            copy = nc.vector.tensor_copy if (gate, s) == half_gates[0] else nc.scalar.copy
-            codes[gate, s] = keep.tile([P, 2 * HALF], U32, name="codes_%s%d" % (gate, s), align_bytes=64)
-            scales[gate, s] = keep.tile([P, 2 * HALF], U8, name="scales_%s%d" % (gate, s), align_bytes=64)
-            for number in range(len(sides)):
+        def flip_weights(gate, s):
+            words = weight_rows[gate, s][:].bitcast(F32)
+            for number, side in enumerate(sides):
+                grouped[gate, s, side] = flip_two_blocks(nc, flip, stage, ident, words, 2 * number)
+
+        def quantise_weights(gate, s):
+            codes[gate, s] = keep.tile(
+                [P, 2 * HALF], U32, name="codes_%s%d" % (gate, s), align_bytes=64
+            )
+            scales[gate, s] = keep.tile(
+                [P, 2 * HALF], U8, name="scales_%s%d" % (gate, s), align_bytes=64
+            )
+            for number, side in enumerate(sides):
                 columns = slice(number * HALF, (number + 1) * HALF)
-                quantise_two_blocks(
-                    nc, copy, flip, stage, ident,
-                    weight_rows[gate, s][:].bitcast(F32), 2 * number,
-                    codes[gate, s][:, columns], scales[gate, s][:, columns],
+                nc.vector.quantize_mx(
+                    out=codes[gate, s][:, columns].bitcast(FP8X4),
+                    scales=scales[gate, s][:, columns],
+                    in_=grouped[gate, s, side][:],
                 )
 
-        squashed = {"z": keep.tile([P, H], F32, name="tanh_z"), "o": keep.tile([P, H], F32, name="tanh_o")}
+        squashed = {
+            "z": keep.tile([P, H], F32, name="tanh_z"),
+            "o": keep.tile([P, H], F32, name="tanh_o"),
+        }
 
         def squash(gate, s):
             acc = sums.tile([P, HALF], F32)
@@ -156,35 +173,55 @@ def tile_slstmlayer_pb_s_kernel(
                 scale=(1.0 if gate == "z" else 0.5),
             )
 
+        kept = keep.tile([P, H], F32)
+        nc.gpsimd.tensor_tensor(out=kept[:], in0=f_sb[:], in1=c_sb[:], op=ALU.mult)
         c_t = keep.tile([P, H], F32)
         half_ratio = keep.tile([P, H], F32)
         h_t = keep.tile([P, H], F32)
 
-        def finish(gate, s):
+        def cell(s):
             outputs = slice(s * HALF, (s + 1) * HALF)
-            if gate == "z":
-                kept = stage.tile([P, HALF], F32)
-                nc.vector.tensor_tensor(out=kept[:], in0=f_sb[:, outputs], in1=c_sb[:, outputs], op=ALU.mult)
-                fresh = stage.tile([P, HALF], F32)
-                nc.vector.tensor_tensor(out=fresh[:], in0=i_sb[:, outputs], in1=squashed["z"][:, outputs], op=ALU.mult)
-                nc.vector.tensor_tensor(out=c_t[:, outputs], in0=kept[:], in1=fresh[:], op=ALU.add)
-                nc.sync.dma_start(out=out_1[:, outputs], in_=c_t[:, outputs])
-                nc.vector.scalar_tensor_tensor(
-                    out=half_ratio[:, outputs], in0=c_t[:, outputs], scalar=0.5,
-                    in1=n_inverse[:, outputs], op0=ALU.mult, op1=ALU.mult,
-                )
-            else:
-                nc.vector.scalar_tensor_tensor(
-                    out=h_t[:, outputs], in0=squashed["o"][:, outputs], scalar=1.0,
-                    in1=half_ratio[:, outputs], op0=ALU.add, op1=ALU.mult,
-                )
-                nc.sync.dma_start(out=out_0[:, outputs], in_=h_t[:, outputs])
+            fresh = stage.tile([P, HALF], F32)
+            nc.gpsimd.tensor_tensor(
+                out=fresh[:], in0=i_sb[:, outputs], in1=squashed["z"][:, outputs], op=ALU.mult
+            )
+            nc.gpsimd.tensor_tensor(
+                out=c_t[:, outputs], in0=kept[:, outputs], in1=fresh[:], op=ALU.add
+            )
+            nc.sync.dma_start(out=out_1[:, outputs], in_=c_t[:, outputs])
+
+        def ratio(s):
+            outputs = slice(s * HALF, (s + 1) * HALF)
+            nc.vector.scalar_tensor_tensor(
+                out=half_ratio[:, outputs], in0=c_t[:, outputs], scalar=0.5,
+                in1=n_inverse[:, outputs], op0=ALU.mult, op1=ALU.mult,
+            )
+
+        def readout(s):
+            outputs = slice(s * HALF, (s + 1) * HALF)
+            nc.vector.scalar_tensor_tensor(
+                out=h_t[:, outputs], in0=squashed["o"][:, outputs], scalar=1.0,
+                in1=half_ratio[:, outputs], op0=ALU.add, op1=ALU.mult,
+            )
+            nc.sync.dma_start(out=out_0[:, outputs], in_=h_t[:, outputs])
 
         count = len(half_gates)
-        for step in range(-1, count + 1):
+        flip_weights(*half_gates[0])
+        quantise_weights(*half_gates[0])
+        invert(1)
+        for step in range(count + 1):
             if step + 1 < count:
-                prepare(*half_gates[step + 1])
-            if 0 <= step < count:
+                flip_weights(*half_gates[step + 1])
+            if step < count:
                 squash(*half_gates[step])
-            if step >= 1:
-                finish(*half_gates[step - 1])
+            before = half_gates[step - 1] if step >= 1 else None
+            if before and before[0] == "z":
+                cell(before[1])
+            if step + 1 < count:
+                quantise_weights(*half_gates[step + 1])
+            if step + 2 < QUARTERS:
+                invert(step + 2)
+            if before and before[0] == "z":
+                ratio(before[1])
+            if before and before[0] == "o":
+                readout(before[1])

@@ -46,7 +46,7 @@ def tile_slstmlayer_pb_s_kernel(
 
     with ExitStack() as ctx:
         keep = ctx.enter_context(tc.tile_pool(name="keep", bufs=1))
-        stage = ctx.enter_context(tc.tile_pool(name="stage", bufs=4))
+        stage = ctx.enter_context(tc.tile_pool(name="stage", bufs=6))
         flip = ctx.enter_context(tc.psum_pool(name="flip", bufs=6))
         sums = ctx.enter_context(tc.psum_pool(name="sums", bufs=2))
         ctx.enter_context(tc.manual_schedule())
@@ -206,22 +206,23 @@ def tile_slstmlayer_pb_s_kernel(
             nc.sync.dma_start(out=out_0[:, outputs], in_=h_t[:, outputs])
 
         count = len(half_gates)
-        flip_weights(*half_gates[0])
-        quantise_weights(*half_gates[0])
-        invert(1)
-        for step in range(count + 1):
-            if step + 1 < count:
-                flip_weights(*half_gates[step + 1])
-            if step < count:
-                squash(*half_gates[step])
-            before = half_gates[step - 1] if step >= 1 else None
-            if before and before[0] == "z":
-                cell(before[1])
-            if step + 1 < count:
-                quantise_weights(*half_gates[step + 1])
-            if step + 2 < QUARTERS:
+
+        def at(index):
+            return half_gates[index] if 0 <= index < count else None
+
+        for step in range(-2, count + 2):
+            if at(step + 2):
+                flip_weights(*at(step + 2))
+            if 1 <= step + 2 < QUARTERS:
                 invert(step + 2)
-            if before and before[0] == "z":
-                ratio(before[1])
-            if before and before[0] == "o":
-                readout(before[1])
+            if at(step + 1):
+                quantise_weights(*at(step + 1))
+            if at(step):
+                squash(*at(step))
+                if at(step)[0] == "z":
+                    cell(at(step)[1])
+            if at(step - 2):
+                if at(step - 2)[0] == "z":
+                    ratio(at(step - 2)[1])
+                else:
+                    readout(at(step - 2)[1])

@@ -15,23 +15,25 @@ P = 128
 K = 512
 H = 512
 WORDS = K // 2
-HALF = 2 * P
+HALF_GATE = 2 * P
 QUARTERS = 4
+PSUM_BANKS = 8
+SUM_BANKS = 2
 
 FLOPS = 2 * P * (2 * K) * (2 * H)
 
 
-def flip_two_blocks(nc, flip, stage, ident, words, first_block):
-    bank = flip.tile([P, 2 * WORDS], F32)
+def turn_two_panels(nc, turned_pool, grouped_pool, ident, words, first_panel):
+    bank = turned_pool.tile([P, 2 * WORDS], F32)
     for piece in range(4):
-        source = first_block * WORDS + piece * P
+        source = first_panel * WORDS + piece * P
         nc.tensor.transpose(
             bank[:, piece * P : (piece + 1) * P], words[:, source : source + P], ident[:]
         )
-    grouped = stage.tile([P, 4 * HALF], BF16, align_bytes=64)
+    grouped = grouped_pool.tile([P, 4 * HALF_GATE], BF16, align_bytes=64)
     nc.scalar.copy(
-        out=grouped[:].bitcast(F32).rearrange("q (s c u) -> q s c u", s=2, u=2),
-        in_=bank[:].rearrange("q (s u c) -> q s c u", s=2, u=2),
+        out=grouped[:].bitcast(F32).rearrange("q (a c u) -> q a c u", a=2, u=2),
+        in_=bank[:].rearrange("q (a u c) -> q a c u", a=2, u=2),
     )
     return grouped
 
@@ -47,11 +49,11 @@ def tile_slstmlayer_pb_s_kernel(
     with ExitStack() as ctx:
         keep = ctx.enter_context(tc.tile_pool(name="keep", bufs=1))
         stage = ctx.enter_context(tc.tile_pool(name="stage", bufs=6))
-        flip = ctx.enter_context(tc.psum_pool(name="flip", bufs=6))
-        sums = ctx.enter_context(tc.psum_pool(name="sums", bufs=2))
+        turned_pool = ctx.enter_context(tc.psum_pool(name="turned", bufs=PSUM_BANKS - SUM_BANKS))
+        sums = ctx.enter_context(tc.psum_pool(name="sums", bufs=SUM_BANKS))
         ctx.enter_context(tc.manual_schedule())
 
-        bias_rows = keep.tile([P, HALF], BF16)
+        bias_rows = keep.tile([P, 2 * P], BF16)
         nc.gpsimd.memset(bias_rows[:].bitcast(F32), 0.0)
         ident = keep.tile([P, P], F32)
         make_identity(nc, ident[:])
@@ -75,28 +77,27 @@ def tile_slstmlayer_pb_s_kernel(
         weight_rows = {}
         for gate, s in half_gates:
             rows = keep.tile([P, 4 * K], BF16, name="rows_%s%d" % (gate, s))
-            for number, side in enumerate(sides):
+            for side_index, side in enumerate(sides):
                 nc.sync.dma_start(
-                    out=rows[:, number * 2 * K : (number + 1) * 2 * K],
+                    out=rows[:, side_index * 2 * K : (side_index + 1) * 2 * K],
                     in_=weights[gate, side].rearrange("(s p j) k -> s p (j k)", s=2, j=2)[s],
                 )
             weight_rows[gate, s] = rows
-            if (gate, s) == ("z", 1):
-                c_sb = load_rows("c_sb", c_prev)
+        c_sb = load_rows("c_sb", c_prev)
 
-        turned = flip.tile([P, 2 * WORDS], F32, tag="bank")
-        nc.tensor.transpose(turned[:, 0:P], bias_rows[:].bitcast(F32), ident[:])
+        bias_turned = turned_pool.tile([P, 2 * WORDS], F32, tag="bank")
+        nc.tensor.transpose(bias_turned[:, 0:P], bias_rows[:].bitcast(F32), ident[:])
         bias_words = keep.tile([P, 4], F32)
-        nc.vector.tensor_copy(out=bias_words[:], in_=turned[:, 0:4])
-        spread = flip.tile([P, 2 * WORDS], F32, tag="bank")
+        nc.vector.tensor_copy(out=bias_words[:], in_=bias_turned[:, 0:4])
+        bias_spread = turned_pool.tile([P, 2 * WORDS], F32, tag="bank")
         for r in range(4):
             nc.tensor.transpose(
-                spread[:, r * P : (r + 1) * P],
+                bias_spread[:, r * P : (r + 1) * P],
                 bias_words[:, r : r + 1].to_broadcast([P, P]),
                 ident[:],
             )
         bias_all = keep.tile([P, 2 * H], BF16)
-        nc.scalar.copy(out=bias_all[:].bitcast(F32), in_=spread[:])
+        nc.scalar.copy(out=bias_all[:].bitcast(F32), in_=bias_spread[:])
         bias = {"z": bias_all[:, 0:H], "o": bias_all[:, H : 2 * H]}
 
         n_t = keep.tile([P, H], F32)
@@ -111,9 +112,9 @@ def tile_slstmlayer_pb_s_kernel(
 
         invert(0)
 
-        act_codes = keep.tile([P, HALF], U32, align_bytes=64)
-        act_scales = keep.tile([P, HALF], U8, align_bytes=64)
-        act_grouped = flip_two_blocks(nc, flip, stage, ident, acts[:].bitcast(F32), 0)
+        act_codes = keep.tile([P, 2 * P], U32, align_bytes=64)
+        act_scales = keep.tile([P, 2 * P], U8, align_bytes=64)
+        act_grouped = turn_two_panels(nc, turned_pool, stage, ident, acts[:].bitcast(F32), 0)
         nc.vector.quantize_mx(
             out=act_codes[:].bitcast(FP8X4), scales=act_scales[:], in_=act_grouped[:]
         )
@@ -122,20 +123,22 @@ def tile_slstmlayer_pb_s_kernel(
         codes = {}
         scales = {}
 
-        def flip_weights(gate, s):
+        def turn_weights(gate, s):
             words = weight_rows[gate, s][:].bitcast(F32)
-            for number, side in enumerate(sides):
-                grouped[gate, s, side] = flip_two_blocks(nc, flip, stage, ident, words, 2 * number)
+            for side_index, side in enumerate(sides):
+                grouped[gate, s, side] = turn_two_panels(
+                    nc, turned_pool, stage, ident, words, 2 * side_index
+                )
 
         def quantise_weights(gate, s):
             codes[gate, s] = keep.tile(
-                [P, 2 * HALF], U32, name="codes_%s%d" % (gate, s), align_bytes=64
+                [P, 2 * HALF_GATE], U32, name="codes_%s%d" % (gate, s), align_bytes=64
             )
             scales[gate, s] = keep.tile(
-                [P, 2 * HALF], U8, name="scales_%s%d" % (gate, s), align_bytes=64
+                [P, 2 * HALF_GATE], U8, name="scales_%s%d" % (gate, s), align_bytes=64
             )
-            for number, side in enumerate(sides):
-                columns = slice(number * HALF, (number + 1) * HALF)
+            for side_index, side in enumerate(sides):
+                columns = slice(side_index * HALF_GATE, (side_index + 1) * HALF_GATE)
                 nc.vector.quantize_mx(
                     out=codes[gate, s][:, columns].bitcast(FP8X4),
                     scales=scales[gate, s][:, columns],
@@ -148,20 +151,20 @@ def tile_slstmlayer_pb_s_kernel(
         }
 
         def squash(gate, s):
-            acc = sums.tile([P, HALF], F32)
-            for number in range(len(sides)):
-                columns = slice(number * HALF, (number + 1) * HALF)
+            acc = sums.tile([P, HALF_GATE], F32)
+            for side_index in range(len(sides)):
+                columns = slice(side_index * HALF_GATE, (side_index + 1) * HALF_GATE)
                 nc.tensor.matmul_mx(
                     out=acc[:],
-                    lhsT=act_codes[:, number * P : (number + 1) * P].bitcast(FP8X4),
-                    lhsT_scale=act_scales[:, number * P : (number + 1) * P],
+                    lhsT=act_codes[:, side_index * P : (side_index + 1) * P].bitcast(FP8X4),
+                    lhsT_scale=act_scales[:, side_index * P : (side_index + 1) * P],
                     rhs=codes[gate, s][:, columns].bitcast(FP8X4),
                     rhs_scale=scales[gate, s][:, columns],
-                    start=(number == 0),
-                    stop=(number == len(sides) - 1),
+                    start=(side_index == 0),
+                    stop=(side_index == len(sides) - 1),
                 )
-            outputs = slice(s * HALF, (s + 1) * HALF)
-            affine = stage.tile([P, HALF], F32)
+            outputs = slice(s * HALF_GATE, (s + 1) * HALF_GATE)
+            affine = stage.tile([P, HALF_GATE], F32)
             nc.vector.tensor_tensor(
                 out=affine[:].rearrange("b (p j) -> b p j", j=2),
                 in0=acc[:].rearrange("b (j p) -> b p j", j=2),
@@ -176,12 +179,12 @@ def tile_slstmlayer_pb_s_kernel(
         kept = keep.tile([P, H], F32)
         nc.gpsimd.tensor_tensor(out=kept[:], in0=f_sb[:], in1=c_sb[:], op=ALU.mult)
         c_t = keep.tile([P, H], F32)
-        half_ratio = keep.tile([P, H], F32)
+        scaled_cell = keep.tile([P, H], F32)
         h_t = keep.tile([P, H], F32)
 
         def cell(s):
-            outputs = slice(s * HALF, (s + 1) * HALF)
-            fresh = stage.tile([P, HALF], F32)
+            outputs = slice(s * HALF_GATE, (s + 1) * HALF_GATE)
+            fresh = stage.tile([P, HALF_GATE], F32)
             nc.gpsimd.tensor_tensor(
                 out=fresh[:], in0=i_sb[:, outputs], in1=squashed["z"][:, outputs], op=ALU.mult
             )
@@ -190,18 +193,18 @@ def tile_slstmlayer_pb_s_kernel(
             )
             nc.sync.dma_start(out=out_1[:, outputs], in_=c_t[:, outputs])
 
-        def ratio(s):
-            outputs = slice(s * HALF, (s + 1) * HALF)
+        def scale_cell(s):
+            outputs = slice(s * HALF_GATE, (s + 1) * HALF_GATE)
             nc.vector.scalar_tensor_tensor(
-                out=half_ratio[:, outputs], in0=c_t[:, outputs], scalar=0.5,
+                out=scaled_cell[:, outputs], in0=c_t[:, outputs], scalar=0.5,
                 in1=n_inverse[:, outputs], op0=ALU.mult, op1=ALU.mult,
             )
 
         def readout(s):
-            outputs = slice(s * HALF, (s + 1) * HALF)
+            outputs = slice(s * HALF_GATE, (s + 1) * HALF_GATE)
             nc.vector.scalar_tensor_tensor(
                 out=h_t[:, outputs], in0=squashed["o"][:, outputs], scalar=1.0,
-                in1=half_ratio[:, outputs], op0=ALU.add, op1=ALU.mult,
+                in1=scaled_cell[:, outputs], op0=ALU.add, op1=ALU.mult,
             )
             nc.sync.dma_start(out=out_0[:, outputs], in_=h_t[:, outputs])
 
@@ -210,19 +213,19 @@ def tile_slstmlayer_pb_s_kernel(
         def at(index):
             return half_gates[index] if 0 <= index < count else None
 
-        for step in range(-2, count + 2):
-            if at(step + 2):
-                flip_weights(*at(step + 2))
-            if 1 <= step + 2 < QUARTERS:
-                invert(step + 2)
-            if at(step + 1):
-                quantise_weights(*at(step + 1))
-            if at(step):
-                squash(*at(step))
-                if at(step)[0] == "z":
-                    cell(at(step)[1])
-            if at(step - 2):
-                if at(step - 2)[0] == "z":
-                    ratio(at(step - 2)[1])
+        for tick in range(count + 4):
+            if at(tick):
+                turn_weights(*at(tick))
+            if 1 <= tick < QUARTERS:
+                invert(tick)
+            if at(tick - 1):
+                quantise_weights(*at(tick - 1))
+            if at(tick - 2):
+                squash(*at(tick - 2))
+                if at(tick - 2)[0] == "z":
+                    cell(at(tick - 2)[1])
+            if at(tick - 4):
+                if at(tick - 4)[0] == "z":
+                    scale_cell(at(tick - 4)[1])
                 else:
-                    readout(at(step - 2)[1])
+                    readout(at(tick - 4)[1])

from contextlib import ExitStack

import concourse.mybir as mybir
from concourse.masks import make_identity

F32 = mybir.dt.float32
BF16 = mybir.dt.bfloat16
U32 = mybir.dt.uint32
U8 = mybir.dt.uint8
FP8X4 = mybir.dt.float8_e4m3fn_x4
ALU = mybir.AluOpType
ACT = mybir.ActivationFunctionType

P = 128
K = 512
H = 512
WORDS = K // 2
HALF_GATE = 2 * P
QUARTERS = 4
PSUM_BANKS = 8
SUM_BANKS = 2

FLOPS = 2 * P * (2 * K) * (2 * H)


def turn_two_panels(nc, turned_pool, grouped_pool, ident, words, first_panel):
    bank = turned_pool.tile([P, 2 * WORDS], F32)
    for piece in range(4):
        source = first_panel * WORDS + piece * P
        nc.tensor.transpose(
            bank[:, piece * P : (piece + 1) * P], words[:, source : source + P], ident[:]
        )
    grouped = grouped_pool.tile([P, 4 * HALF_GATE], BF16, align_bytes=64)
    nc.scalar.copy(
        out=grouped[:].bitcast(F32).rearrange("q (a c u) -> q a c u", a=2, u=2),
        in_=bank[:].rearrange("q (a u c) -> q a c u", a=2, u=2),
    )
    return grouped


def tile_slstmlayer_pb_s_kernel(
    tc, x, h_prev, c_prev, n_prev, i_prime, f_prime, Wz_x, b_z, Wz_h, Wo_x, b_o, Wo_h, out_0, out_1
):
    nc = tc.nc
    half_gates = (("z", 0), ("z", 1), ("o", 0), ("o", 1))
    weights = {("z", "x"): Wz_x, ("z", "h"): Wz_h, ("o", "x"): Wo_x, ("o", "h"): Wo_h}
    sides = ("x", "h")

    with ExitStack() as ctx:
        keep = ctx.enter_context(tc.tile_pool(name="keep", bufs=1))
        stage = ctx.enter_context(tc.tile_pool(name="stage", bufs=6))
        turned_pool = ctx.enter_context(tc.psum_pool(name="turned", bufs=PSUM_BANKS - SUM_BANKS))
        sums = ctx.enter_context(tc.psum_pool(name="sums", bufs=SUM_BANKS))
        ctx.enter_context(tc.manual_schedule())

        bias_rows = keep.tile([P, 2 * P], BF16)
        nc.gpsimd.memset(bias_rows[:].bitcast(F32), 0.0)
        ident = keep.tile([P, P], F32)
        make_identity(nc, ident[:])

        nc.sync.dma_start(out=bias_rows[0:2, :], in_=b_z.rearrange("(r c) -> r c", r=2))
        nc.sync.dma_start(out=bias_rows[2:4, :], in_=b_o.rearrange("(r c) -> r c", r=2))

        def load_rows(name, source):
            rows = keep.tile([P, H], BF16, name=name)
            nc.sync.dma_start(out=rows[:], in_=source)
            return rows

        f_sb = load_rows("f_sb", f_prime)
        n_sb = load_rows("n_sb", n_prev)
        i_sb = load_rows("i_sb", i_prime)

        acts = keep.tile([P, 2 * K], BF16)
        nc.sync.dma_start(out=acts[:, 0:K], in_=x)
        nc.sync.dma_start(out=acts[:, K : 2 * K], in_=h_prev)

        weight_rows = {}
        for gate, s in half_gates:
            rows = keep.tile([P, 4 * K], BF16, name="rows_%s%d" % (gate, s))
            for side_index, side in enumerate(sides):
                nc.sync.dma_start(
                    out=rows[:, side_index * 2 * K : (side_index + 1) * 2 * K],
                    in_=weights[gate, side].rearrange("(s p j) k -> s p (j k)", s=2, j=2)[s],
                )
            weight_rows[gate, s] = rows
        c_sb = load_rows("c_sb", c_prev)

        bias_turned = turned_pool.tile([P, 2 * WORDS], F32, tag="bank")
        nc.tensor.transpose(bias_turned[:, 0:P], bias_rows[:].bitcast(F32), ident[:])
        bias_words = keep.tile([P, 4], F32)
        nc.vector.tensor_copy(out=bias_words[:], in_=bias_turned[:, 0:4])
        bias_spread = turned_pool.tile([P, 2 * WORDS], F32, tag="bank")
        for r in range(4):
            nc.tensor.transpose(
                bias_spread[:, r * P : (r + 1) * P],
                bias_words[:, r : r + 1].to_broadcast([P, P]),
                ident[:],
            )
        bias_all = keep.tile([P, 2 * H], BF16)
        nc.scalar.copy(out=bias_all[:].bitcast(F32), in_=bias_spread[:])
        bias = {"z": bias_all[:, 0:H], "o": bias_all[:, H : 2 * H]}

        n_t = keep.tile([P, H], F32)
        nc.vector.tensor_tensor(out=n_t[:], in0=f_sb[:], in1=n_sb[:], op=ALU.mult)
        nc.vector.tensor_tensor(out=n_t[:], in0=n_t[:], in1=i_sb[:], op=ALU.add)
        nc.vector.tensor_scalar_max(out=n_t[:], in0=n_t[:], scalar1=1e-6)
        n_inverse = keep.tile([P, H], F32)

        def invert(quarter):
            columns = slice(quarter * H // QUARTERS, (quarter + 1) * H // QUARTERS)
            nc.vector.reciprocal(out=n_inverse[:, columns], in_=n_t[:, columns])

        invert(0)

        act_codes = keep.tile([P, 2 * P], U32, align_bytes=64)
        act_scales = keep.tile([P, 2 * P], U8, align_bytes=64)
        act_grouped = turn_two_panels(nc, turned_pool, stage, ident, acts[:].bitcast(F32), 0)
        nc.vector.quantize_mx(
            out=act_codes[:].bitcast(FP8X4), scales=act_scales[:], in_=act_grouped[:]
        )

        grouped = {}
        codes = {}
        scales = {}

        def turn_weights(gate, s):
            words = weight_rows[gate, s][:].bitcast(F32)
            for side_index, side in enumerate(sides):
                grouped[gate, s, side] = turn_two_panels(
                    nc, turned_pool, stage, ident, words, 2 * side_index
                )

        def quantise_weights(gate, s):
            codes[gate, s] = keep.tile(
                [P, 2 * HALF_GATE], U32, name="codes_%s%d" % (gate, s), align_bytes=64
            )
            scales[gate, s] = keep.tile(
                [P, 2 * HALF_GATE], U8, name="scales_%s%d" % (gate, s), align_bytes=64
            )
            for side_index, side in enumerate(sides):
                columns = slice(side_index * HALF_GATE, (side_index + 1) * HALF_GATE)
                nc.vector.quantize_mx(
                    out=codes[gate, s][:, columns].bitcast(FP8X4),
                    scales=scales[gate, s][:, columns],
                    in_=grouped[gate, s, side][:],
                )

        squashed = {
            "z": keep.tile([P, H], F32, name="tanh_z"),
            "o": keep.tile([P, H], F32, name="tanh_o"),
        }

        def squash(gate, s):
            acc = sums.tile([P, HALF_GATE], F32)
            for side_index in range(len(sides)):
                columns = slice(side_index * HALF_GATE, (side_index + 1) * HALF_GATE)
                nc.tensor.matmul_mx(
                    out=acc[:],
                    lhsT=act_codes[:, side_index * P : (side_index + 1) * P].bitcast(FP8X4),
                    lhsT_scale=act_scales[:, side_index * P : (side_index + 1) * P],
                    rhs=codes[gate, s][:, columns].bitcast(FP8X4),
                    rhs_scale=scales[gate, s][:, columns],
                    start=(side_index == 0),
                    stop=(side_index == len(sides) - 1),
                )
            outputs = slice(s * HALF_GATE, (s + 1) * HALF_GATE)
            affine = stage.tile([P, HALF_GATE], F32)
            nc.vector.tensor_tensor(
                out=affine[:].rearrange("b (p j) -> b p j", j=2),
                in0=acc[:].rearrange("b (j p) -> b p j", j=2),
                in1=bias[gate][:, outputs].rearrange("b (p j) -> b p j", j=2),
                op=ALU.add,
            )
            nc.scalar.activation(
                out=squashed[gate][:, outputs], in_=affine[:], func=ACT.Tanh,
                scale=(1.0 if gate == "z" else 0.5),
            )

        kept = keep.tile([P, H], F32)
        nc.gpsimd.tensor_tensor(out=kept[:], in0=f_sb[:], in1=c_sb[:], op=ALU.mult)
        c_t = keep.tile([P, H], F32)
        scaled_cell = keep.tile([P, H], F32)
        h_t = keep.tile([P, H], F32)

        def cell(s):
            outputs = slice(s * HALF_GATE, (s + 1) * HALF_GATE)
            fresh = stage.tile([P, HALF_GATE], F32)
            nc.gpsimd.tensor_tensor(
                out=fresh[:], in0=i_sb[:, outputs], in1=squashed["z"][:, outputs], op=ALU.mult
            )
            nc.gpsimd.tensor_tensor(
                out=c_t[:, outputs], in0=kept[:, outputs], in1=fresh[:], op=ALU.add
            )
            nc.sync.dma_start(out=out_1[:, outputs], in_=c_t[:, outputs])

        def scale_cell(s):
            outputs = slice(s * HALF_GATE, (s + 1) * HALF_GATE)
            nc.vector.scalar_tensor_tensor(
                out=scaled_cell[:, outputs], in0=c_t[:, outputs], scalar=0.5,
                in1=n_inverse[:, outputs], op0=ALU.mult, op1=ALU.mult,
            )

        def readout(s):
            outputs = slice(s * HALF_GATE, (s + 1) * HALF_GATE)
            nc.vector.scalar_tensor_tensor(
                out=h_t[:, outputs], in0=squashed["o"][:, outputs], scalar=1.0,
                in1=scaled_cell[:, outputs], op0=ALU.add, op1=ALU.mult,
            )
            nc.sync.dma_start(out=out_0[:, outputs], in_=h_t[:, outputs])

        count = len(half_gates)

        def at(index):
            return half_gates[index] if 0 <= index < count else None

        for tick in range(count + 4):
            if at(tick):
                turn_weights(*at(tick))
            if 1 <= tick < QUARTERS:
                invert(tick)
            if at(tick - 1):
                quantise_weights(*at(tick - 1))
            if at(tick - 2):
                squash(*at(tick - 2))
                if at(tick - 2)[0] == "z":
                    cell(at(tick - 2)[1])
            if at(tick - 4):
                if at(tick - 4)[0] == "z":
                    scale_cell(at(tick - 4)[1])
                else:
                    readout(at(tick - 4)[1])
